import numpy as np
import ml_dtypes


def mxq(x, axis, fmt="e4m3"):
    dtype, down = {"e4m3": (ml_dtypes.float8_e4m3fn, 7), "e5m2": (ml_dtypes.float8_e5m2, 14)}[fmt]
    v = np.moveaxis(np.asarray(x, np.float32).astype(ml_dtypes.bfloat16).astype(np.float64), axis, -1)
    blocks = v.reshape(v.shape[:-1] + (-1, 32))
    amax = np.abs(blocks).max(-1, keepdims=True)
    byte = np.maximum(np.where(amax > 0, np.frexp(amax)[1] - 1 + 127, 0) - down, 1)
    scale = np.exp2(byte - 127.0)
    codes = (blocks / scale).astype(np.float32).astype(dtype).astype(np.float64)
    return np.moveaxis((codes * scale).reshape(v.shape), -1, axis)


WIDE = False


def mx_kscale(k):
    if not WIDE:
        return np.ones(k)
    levels = np.array([10, -10, 5, -5, 0])
    if k % 512:
        return np.exp2(np.random.permutation(np.resize(levels, k // 32))).repeat(32)
    a = np.empty((k // 512, 16))
    for p in range(k // 512):
        a[p, :8] = np.random.permutation(np.resize(levels, 8))
        for g in range(8):
            far = levels[np.abs(levels - a[p, g]) >= 10]
            a[p, g + 8] = far[np.random.randint(len(far))]
    return np.exp2(a.ravel()).repeat(32)


BF16 = ml_dtypes.bfloat16


def bf(x):
    return np.asarray(x, np.float32).astype(BF16)


def f64(x):
    return np.asarray(x).astype(np.float64)


N, DIN, H1, H2, C, NC, G = 1024, 512, 512, 256, 128, 512, 8


def setup_inputs():
    s, t = mx_kscale(N), mx_kscale(DIN)
    return {"F_": bf(np.random.uniform(size=(N, N)) * 2.0 / np.sqrt(N) * s),
            "X": bf(np.random.standard_normal((N, DIN)) / s[:, None] * t),
            "W1": bf(np.random.standard_normal((DIN, H1)) * 0.8 / np.sqrt(DIN) / t[:, None]),
            "b1": bf(np.random.standard_normal(H1) * 0.3)}


def reference(F_, X, W1, b1):
    agg = mxq(f64(F_), 1, "e4m3") @ mxq(f64(X), 0, "e4m3")
    return np.tanh((mxq(agg, 1, "e4m3") @ mxq(f64(W1), 0, "e4m3")) + f64(b1))

@@ -1,0 +1,208 @@
+from contextlib import ExitStack
+
+import concourse.mybir as mybir
+from concourse.masks import make_identity
+
+F32 = mybir.dt.float32
+BF16 = mybir.dt.bfloat16
+U32 = mybir.dt.uint32
+U8 = mybir.dt.uint8
+FP8X4 = mybir.dt.float8_e4m3fn_x4
+
+P = 128
+PACK = 4
+K_PASS = P * PACK
+NODES = 1024
+FEATS = 512
+HIDDEN = 512
+BLOCKS = NODES // P
+PASSES = NODES // K_PASS
+FEAT_TILES = FEATS // P
+GROUP = 2
+GROUPS = BLOCKS // GROUP
+AGG_LAG = 1
+OUT_LAG = 3
+
+FLOPS = 2 * NODES * NODES * FEATS + 2 * NODES * FEATS * HIDDEN
+
+
+def tile_controencodnet_pa_kernel(tc, F_, X, W1, b1, out):
+    nc = tc.nc
+    with ExitStack() as ctx:
+        keep = ctx.enter_context(tc.tile_pool(name="keep", bufs=1))
+        psum_f = ctx.enter_context(tc.psum_pool(name="psum_f", bufs=2 * GROUP))
+        psum_a = ctx.enter_context(tc.psum_pool(name="psum_a", bufs=GROUP))
+        psum_o = ctx.enter_context(tc.psum_pool(name="psum_o", bufs=GROUP))
+        ctx.enter_context(tc.manual_schedule())
+
+        f_in = keep.tile([P, BLOCKS, NODES], BF16)
+        x_in = keep.tile([P, PASSES, PACK, FEATS], BF16)
+        w_in = keep.tile([P, PACK, HIDDEN], BF16)
+        f_grouped = keep.tile([P, BLOCKS, PASSES * P * PACK], BF16, align_bytes=64)
+        x_grouped = keep.tile([P, PASSES, FEATS, PACK], BF16, align_bytes=64)
+        w_grouped = keep.tile([P, HIDDEN, PACK], BF16, align_bytes=64)
+        a_grouped = keep.tile([P, BLOCKS, P, PACK], BF16, align_bytes=64)
+        f_codes = keep.tile([P, BLOCKS, PASSES * P], U32, align_bytes=64)
+        f_scales = keep.tile([P, BLOCKS, PASSES * P], U8, align_bytes=64)
+        x_codes = keep.tile([P, PASSES, FEATS], U32, align_bytes=64)
+        x_scales = keep.tile([P, PASSES, FEATS], U8, align_bytes=64)
+        w_codes = keep.tile([P, HIDDEN], U32, align_bytes=64)
+        w_scales = keep.tile([P, HIDDEN], U8, align_bytes=64)
+        a_codes = keep.tile([P, BLOCKS, P], U32, align_bytes=64)
+        a_scales = keep.tile([P, BLOCKS, P], U8, align_bytes=64)
+        result = keep.tile([P, BLOCKS, HIDDEN], F32)
+
+        identity = keep.tile([P, P], F32)
+        ones = keep.tile([P, P], BF16)
+        bias_row = keep.tile([P, HIDDEN], BF16)
+        bias_all = keep.tile([P, HIDDEN], F32)
+        warm = keep.tile([P, 1], F32)
+
+        f_rows = F_.rearrange("(n r) k -> n r k", r=BLOCKS)
+        out_rows = out.rearrange("(n r) c -> n r c", r=BLOCKS)
+
+        x_rows = X.rearrange("(g p t) c -> g p t c", g=PASSES, t=PACK)
+        def load_f(first, count):
+            blocks = slice(first, first + count)
+            nc.sync.dma_start(out=f_in[:, blocks, :], in_=f_rows[:, blocks, :])
+
+        for g in range(PASSES):
+            for u in range(2):
+                nc.sync.dma_start(out=x_in[:, g, 2 * u : 2 * u + 2, :], in_=x_rows[g, :, 2 * u : 2 * u + 2, :])
+            load_f(g, 1)
+        load_f(PASSES, GROUP)
+        nc.sync.dma_start(out=w_in[:], in_=W1.rearrange("(p t) c -> p t c", t=PACK))
+        for first in range(PASSES + GROUP, BLOCKS, GROUP):
+            load_f(first, GROUP)
+
+        nc.vector.memset(bias_row[:], 0.0)
+        nc.scalar.dma_start(out=bias_row[0:1, :], in_=b1.rearrange("(o c) -> o c", o=1))
+        nc.vector.memset(ones[:], 1.0)
+        nc.vector.memset(warm[:], 0.0)
+        nc.scalar.activation(out=warm[:], in_=warm[:], func=mybir.ActivationFunctionType.Tanh)
+        make_identity(nc, identity[:])
+
+        def regroup(grouped, rows):
+            nc.vector.tensor_copy(
+                out=grouped.rearrange("p (c i) t -> p c t i", i=4),
+                in_=rows.rearrange("p t (c i) -> p c t i", i=4),
+            )
+
+        def regroup_w(half):
+            cols = slice(half * (HIDDEN // 2), (half + 1) * (HIDDEN // 2))
+            regroup(w_grouped[:, cols, :], w_in[:, :, cols])
+
+        def quantise(codes, scales, grouped):
+            nc.vector.quantize_mx(out=codes.bitcast(FP8X4), scales=scales, in_=grouped)
+
+        def spread_bias():
+            bank = psum_o.tile([P, HIDDEN], F32, tag="o")
+            nc.tensor.matmul(out=bank[:], lhsT=ones[:], rhs=bias_row[:], start=True, stop=True)
+            nc.scalar.copy(out=bias_all[:], in_=bank[:])
+
+        f_banks = {}
+
+        def transpose_f(r):
+            words = f_in[:, r, :].bitcast(F32)
+            bank = psum_f.tile([P, PASSES * 2, P], F32, tag="f")
+            for g in range(PASSES):
+                for u in range(2):
+                    chosen = words[:, g * 2 * P + u : (g + 1) * 2 * P : 2]
+                    nc.tensor.transpose(bank[:, 2 * g + u, :], chosen, identity[:])
+            f_banks[r] = bank
+
+        def quantise_f(r):
+            nc.scalar.copy(
+                out=f_grouped[:, r, :].bitcast(F32).rearrange("p (g n u) -> p g n u", g=PASSES, u=2),
+                in_=f_banks[r][:].rearrange("p (g u) n -> p g n u", u=2),
+            )
+            quantise(f_codes[:, r, :], f_scales[:, r, :], f_grouped[:, r, :])
+
+        a_banks = {}
+
+        def aggregate(r):
+            bank = psum_a.tile([P, FEAT_TILES, P], F32, tag="a")
+            for t in range(FEAT_TILES):
+                feats = slice(t * P, (t + 1) * P)
+                for g in range(PASSES):
+                    nodes = slice(g * P, (g + 1) * P)
+                    nc.tensor.matmul_mx(
+                        out=bank[:, t, :],
+                        lhsT=x_codes[:, g, feats].bitcast(FP8X4),
+                        lhsT_scale=x_scales[:, g, feats],
+                        rhs=f_codes[:, r, nodes].bitcast(FP8X4),
+                        rhs_scale=f_scales[:, r, nodes],
+                        start=(g == 0),
+                        stop=(g == PASSES - 1),
+                    )
+            a_banks[r] = bank
+
+        def round_agg(r):
+            hopping = a_banks[r][:].rearrange("p t n -> p n t")
+            if r < BLOCKS - 1:
+                nc.scalar.copy(out=a_grouped[:, r], in_=hopping)
+            else:
+                nc.vector.tensor_copy(out=a_grouped[:, r], in_=hopping)
+
+        def quantise_agg(r):
+            quantise(
+                a_codes[:, r, :], a_scales[:, r, :], a_grouped[:, r].rearrange("p n t -> p (n t)")
+            )
+
+        def project(r):
+            bank = psum_o.tile([P, HIDDEN], F32, tag="o")
+            nc.tensor.matmul_mx(
+                out=bank[:],
+                lhsT=a_codes[:, r, :].bitcast(FP8X4),
+                lhsT_scale=a_scales[:, r, :],
+                rhs=w_codes[:].bitcast(FP8X4),
+                rhs_scale=w_scales[:],
+                start=True,
+                stop=True,
+            )
+            nc.vector.tensor_tensor(
+                out=result[:, r, :], in0=bank[:], in1=bias_all[:], op=mybir.AluOpType.add
+            )
+
+        def finish(r):
+            nc.scalar.activation(
+                out=result[:, r, :], in_=result[:, r, :], func=mybir.ActivationFunctionType.Tanh
+            )
+            nc.sync.dma_start(out=out_rows[:, r, :], in_=result[:, r, :])
+
+        def blocks_of(group):
+            if 0 <= group < GROUPS:
+                return range(group * GROUP, (group + 1) * GROUP)
+            return range(0)
+
+        for g in range(PASSES):
+            nc.vector.tensor_copy(
+                out=x_grouped[:, g].rearrange("p (t m) j -> p t m j", t=FEAT_TILES),
+                in_=x_in[:, g].rearrange("p j (m t) -> p t m j", t=FEAT_TILES),
+            )
+            quantise(
+                x_codes[:, g, :], x_scales[:, g, :], x_grouped[:, g].rearrange("p c t -> p (c t)")
+            )
+
+        for step in range(GROUPS + OUT_LAG):
+            for r in blocks_of(step):
+                transpose_f(r)
+            for r in blocks_of(step - OUT_LAG):
+                project(r)
+            for r in blocks_of(step):
+                quantise_f(r)
+            if step == 0:
+                spread_bias()
+            if step == AGG_LAG:
+                regroup_w(0)
+            for r in blocks_of(step - AGG_LAG):
+                aggregate(r)
+            for r in blocks_of(step - AGG_LAG):
+                round_agg(r)
+            for r in blocks_of(step - AGG_LAG):
+                quantise_agg(r)
+            for r in blocks_of(step - OUT_LAG):
+                finish(r)
+            if step == AGG_LAG:
+                regroup_w(1)
+                quantise(w_codes[:], w_scales[:], w_grouped[:].rearrange("p c t -> p (c t)"))

@@ -8,6 +8,8 @@ BF16 = mybir.dt.bfloat16
 U32 = mybir.dt.uint32
 U8 = mybir.dt.uint8
 FP8X4 = mybir.dt.float8_e4m3fn_x4
+TANH = mybir.ActivationFunctionType.Tanh
+ADD = mybir.AluOpType.add
 
 P = 128
 PACK = 4
@@ -18,9 +20,7 @@ HIDDEN = 512
 BLOCKS = NODES // P
 PASSES = NODES // K_PASS
 FEAT_TILES = FEATS // P
-GROUP = 2
-GROUPS = BLOCKS // GROUP
-AGG_LAG = 1
+AHEAD = 4
 OUT_LAG = 3
 
 FLOPS = 2 * NODES * NODES * FEATS + 2 * NODES * FEATS * HIDDEN
@@ -30,9 +30,7 @@ def tile_controencodnet_pa_kernel(tc, F_, X, W1, b1, out):
     nc = tc.nc
     with ExitStack() as ctx:
         keep = ctx.enter_context(tc.tile_pool(name="keep", bufs=1))
-        psum_f = ctx.enter_context(tc.psum_pool(name="psum_f", bufs=2 * GROUP))
-        psum_a = ctx.enter_context(tc.psum_pool(name="psum_a", bufs=GROUP))
-        psum_o = ctx.enter_context(tc.psum_pool(name="psum_o", bufs=GROUP))
+        psum = ctx.enter_context(tc.psum_pool(name="psum", bufs=8))
         ctx.enter_context(tc.manual_schedule())
 
         f_in = keep.tile([P, BLOCKS, NODES], BF16)
@@ -53,75 +51,96 @@ def tile_controencodnet_pa_kernel(tc, F_, X, W1, b1, out):
         result = keep.tile([P, BLOCKS, HIDDEN], F32)
 
         identity = keep.tile([P, P], F32)
-        ones = keep.tile([P, P], BF16)
-        bias_row = keep.tile([P, HIDDEN], BF16)
-        bias_all = keep.tile([P, HIDDEN], F32)
+        identity_bf16 = keep.tile([P, P], BF16)
+        bias_columns = keep.tile([P, PACK], BF16)
+        bias_all = keep.tile([P, HIDDEN], BF16)
         warm = keep.tile([P, 1], F32)
 
         f_rows = F_.rearrange("(n r) k -> n r k", r=BLOCKS)
         out_rows = out.rearrange("(n r) c -> n r c", r=BLOCKS)
 
+        nc.scalar.dma_start(out=bias_columns[:], in_=b1.rearrange("(p j) -> p j", j=PACK))
+
         x_rows = X.rearrange("(g p t) c -> g p t c", g=PASSES, t=PACK)
+
+        def load_x(g):
+            nc.sync.dma_start(out=x_in[:, g], in_=x_rows[g])
+
         def load_f(first, count):
             blocks = slice(first, first + count)
             nc.sync.dma_start(out=f_in[:, blocks, :], in_=f_rows[:, blocks, :])
 
-        for g in range(PASSES):
-            for u in range(2):
-                nc.sync.dma_start(out=x_in[:, g, 2 * u : 2 * u + 2, :], in_=x_rows[g, :, 2 * u : 2 * u + 2, :])
-            load_f(g, 1)
-        load_f(PASSES, GROUP)
+        load_x(0)
+        load_f(0, 1)
+        load_x(1)
+        load_f(1, 1)
+        load_f(2, 1)
+        load_f(3, 1)
+        load_f(4, 2)
         nc.sync.dma_start(out=w_in[:], in_=W1.rearrange("(p t) c -> p t c", t=PACK))
-        for first in range(PASSES + GROUP, BLOCKS, GROUP):
-            load_f(first, GROUP)
+        load_f(6, 2)
 
-        nc.vector.memset(bias_row[:], 0.0)
-        nc.scalar.dma_start(out=bias_row[0:1, :], in_=b1.rearrange("(o c) -> o c", o=1))
-        nc.vector.memset(ones[:], 1.0)
         nc.vector.memset(warm[:], 0.0)
-        nc.scalar.activation(out=warm[:], in_=warm[:], func=mybir.ActivationFunctionType.Tanh)
+        nc.scalar.activation(out=warm[:], in_=warm[:], func=TANH)
         make_identity(nc, identity[:])
-
-        def regroup(grouped, rows):
-            nc.vector.tensor_copy(
-                out=grouped.rearrange("p (c i) t -> p c t i", i=4),
-                in_=rows.rearrange("p t (c i) -> p c t i", i=4),
-            )
-
-        def regroup_w(half):
-            cols = slice(half * (HIDDEN // 2), (half + 1) * (HIDDEN // 2))
-            regroup(w_grouped[:, cols, :], w_in[:, :, cols])
+        nc.vector.tensor_copy(out=identity_bf16[:], in_=identity[:])
 
         def quantise(codes, scales, grouped):
             nc.vector.quantize_mx(out=codes.bitcast(FP8X4), scales=scales, in_=grouped)
 
-        def spread_bias():
-            bank = psum_o.tile([P, HIDDEN], F32, tag="o")
-            nc.tensor.matmul(out=bank[:], lhsT=ones[:], rhs=bias_row[:], start=True, stop=True)
-            nc.scalar.copy(out=bias_all[:], in_=bank[:])
+        def regroup_x(g):
+            grouped = x_grouped[:, g].rearrange("p (t m) j -> p t m j", t=FEAT_TILES)
+            rows = x_in[:, g].rearrange("p j (m t) -> p t m j", t=FEAT_TILES)
+            cut = P * 3 // 4
+            nc.scalar.copy(out=grouped[:, :, cut:], in_=rows[:, :, cut:])
+            nc.vector.tensor_copy(out=grouped[:, :, :cut], in_=rows[:, :, :cut])
 
-        f_banks = {}
+        def quantise_x(g):
+            quantise(x_codes[:, g, :], x_scales[:, g, :], x_grouped[:, g].rearrange("p c t -> p (c t)"))
+
+        def regroup_w():
+            nc.vector.tensor_copy(
+                out=w_grouped[:].rearrange("p (c i) t -> p c t i", i=4),
+                in_=w_in[:].rearrange("p t (c i) -> p c t i", i=4),
+            )
+
+        def quantise_w():
+            quantise(w_codes[:], w_scales[:], w_grouped[:].rearrange("p c t -> p (c t)"))
+
+        def spread_bias():
+            bank = psum.tile([P, PACK, P], BF16, tag="bank")
+            for j in range(PACK):
+                nc.tensor.matmul(
+                    out=bank[:, j, :],
+                    lhsT=bias_columns[:, j : j + 1].to_broadcast([P, P]),
+                    rhs=identity_bf16[:],
+                    start=True,
+                    stop=True,
+                )
+            nc.scalar.copy(
+                out=bias_all[:].rearrange("p (n j) -> p n j", j=PACK),
+                in_=bank[:].rearrange("p j n -> p n j"),
+            )
 
         def transpose_f(r):
             words = f_in[:, r, :].bitcast(F32)
-            bank = psum_f.tile([P, PASSES * 2, P], F32, tag="f")
+            bank = psum.tile([P, PASSES * 2, P], F32, tag="bank")
             for g in range(PASSES):
                 for u in range(2):
                     chosen = words[:, g * 2 * P + u : (g + 1) * 2 * P : 2]
                     nc.tensor.transpose(bank[:, 2 * g + u, :], chosen, identity[:])
-            f_banks[r] = bank
-
-        def quantise_f(r):
             nc.scalar.copy(
                 out=f_grouped[:, r, :].bitcast(F32).rearrange("p (g n u) -> p g n u", g=PASSES, u=2),
-                in_=f_banks[r][:].rearrange("p (g u) n -> p g n u", u=2),
+                in_=bank[:].rearrange("p (g u) n -> p g n u", u=2),
             )
+
+        def quantise_f(r):
             quantise(f_codes[:, r, :], f_scales[:, r, :], f_grouped[:, r, :])
 
         a_banks = {}
 
         def aggregate(r):
-            bank = psum_a.tile([P, FEAT_TILES, P], F32, tag="a")
+            bank = psum.tile([P, FEAT_TILES, P], F32, tag="bank")
             for t in range(FEAT_TILES):
                 feats = slice(t * P, (t + 1) * P)
                 for g in range(PASSES):
@@ -139,7 +158,7 @@ def tile_controencodnet_pa_kernel(tc, F_, X, W1, b1, out):
 
         def round_agg(r):
             hopping = a_banks[r][:].rearrange("p t n -> p n t")
-            if r < BLOCKS - 1:
+            if r != 5:
                 nc.scalar.copy(out=a_grouped[:, r], in_=hopping)
             else:
                 nc.vector.tensor_copy(out=a_grouped[:, r], in_=hopping)
@@ -149,8 +168,10 @@ def tile_controencodnet_pa_kernel(tc, F_, X, W1, b1, out):
                 a_codes[:, r, :], a_scales[:, r, :], a_grouped[:, r].rearrange("p n t -> p (n t)")
             )
 
+        o_banks = {}
+
         def project(r):
-            bank = psum_o.tile([P, HIDDEN], F32, tag="o")
+            bank = psum.tile([P, HIDDEN], F32, tag="bank")
             nc.tensor.matmul_mx(
                 out=bank[:],
                 lhsT=a_codes[:, r, :].bitcast(FP8X4),
@@ -160,49 +181,56 @@ def tile_controencodnet_pa_kernel(tc, F_, X, W1, b1, out):
                 start=True,
                 stop=True,
             )
-            nc.vector.tensor_tensor(
-                out=result[:, r, :], in0=bank[:], in1=bias_all[:], op=mybir.AluOpType.add
-            )
+            o_banks[r] = bank
+
+        def parts_of(r):
+            width = HIDDEN // 2 if r == BLOCKS - 1 else HIDDEN
+            return [slice(c, c + width) for c in range(0, HIDDEN, width)]
+
+        def add_bias(r):
+            for cols in parts_of(r):
+                nc.vector.tensor_tensor(
+                    out=result[:, r, cols], in0=o_banks[r][:, cols], in1=bias_all[:, cols], op=ADD
+                )
 
         def finish(r):
-            nc.scalar.activation(
-                out=result[:, r, :], in_=result[:, r, :], func=mybir.ActivationFunctionType.Tanh
-            )
-            nc.sync.dma_start(out=out_rows[:, r, :], in_=result[:, r, :])
+            for cols in parts_of(r):
+                piece = result[:, r, cols]
+                nc.scalar.activation(out=piece, in_=piece, func=TANH)
+                nc.sync.dma_start(out=out_rows[:, r, cols], in_=piece)
 
-        def blocks_of(group):
-            if 0 <= group < GROUPS:
-                return range(group * GROUP, (group + 1) * GROUP)
-            return range(0)
+        regroup_x(0)
+        transpose_f(0)
+        quantise_x(0)
+        regroup_x(1)
+        quantise_f(0)
+        quantise_x(1)
+        transpose_f(1)
+        spread_bias()
+        for r in range(2, AHEAD):
+            transpose_f(r)
+        for r in range(1, AHEAD):
+            quantise_f(r)
 
-        for g in range(PASSES):
-            nc.vector.tensor_copy(
-                out=x_grouped[:, g].rearrange("p (t m) j -> p t m j", t=FEAT_TILES),
-                in_=x_in[:, g].rearrange("p j (m t) -> p t m j", t=FEAT_TILES),
-            )
-            quantise(
-                x_codes[:, g, :], x_scales[:, g, :], x_grouped[:, g].rearrange("p c t -> p (c t)")
-            )
-
-        for step in range(GROUPS + OUT_LAG):
-            for r in blocks_of(step):
-                transpose_f(r)
-            for r in blocks_of(step - OUT_LAG):
-                project(r)
-            for r in blocks_of(step):
-                quantise_f(r)
+        for step in range(BLOCKS + OUT_LAG + 1):
+            done = step - OUT_LAG
+            if step < BLOCKS:
+                aggregate(step)
+                round_agg(step)
+            if step in (0, 2):
+                transpose_f(AHEAD + step)
+                transpose_f(AHEAD + step + 1)
+            if 0 <= done < BLOCKS:
+                project(done)
             if step == 0:
-                spread_bias()
-            if step == AGG_LAG:
-                regroup_w(0)
-            for r in blocks_of(step - AGG_LAG):
-                aggregate(r)
-            for r in blocks_of(step - AGG_LAG):
-                round_agg(r)
-            for r in blocks_of(step - AGG_LAG):
-                quantise_agg(r)
-            for r in blocks_of(step - OUT_LAG):
-                finish(r)
-            if step == AGG_LAG:
-                regroup_w(1)
-                quantise(w_codes[:], w_scales[:], w_grouped[:].rearrange("p c t -> p (c t)"))
+                regroup_w()
+            if 0 <= done < BLOCKS:
+                add_bias(done)
+            if step < BLOCKS:
+                quantise_agg(step)
+            if step + AHEAD < BLOCKS:
+                quantise_f(step + AHEAD)
+            if step == 0:
+                quantise_w()
+            if 0 <= done - 1 < BLOCKS:
+                finish(done - 1)

@@ -107,19 +107,22 @@ def tile_controencodnet_pa_kernel(tc, F_, X, W1, b1, out):
         def quantise_w():
             quantise(w_codes[:], w_scales[:], w_grouped[:].rearrange("p c t -> p (c t)"))
 
+        b_bank = psum.tile([P, PACK, P], BF16, tag="bank")
+
         def spread_bias():
-            bank = psum.tile([P, PACK, P], BF16, tag="bank")
             for j in range(PACK):
                 nc.tensor.matmul(
-                    out=bank[:, j, :],
+                    out=b_bank[:, j, :],
                     lhsT=bias_columns[:, j : j + 1].to_broadcast([P, P]),
                     rhs=identity_bf16[:],
                     start=True,
                     stop=True,
                 )
+
+        def keep_bias():
             nc.scalar.copy(
                 out=bias_all[:].rearrange("p (n j) -> p n j", j=PACK),
-                in_=bank[:].rearrange("p j n -> p n j"),
+                in_=b_bank[:].rearrange("p j n -> p n j"),
             )
 
         def transpose_f(r):
@@ -158,7 +161,7 @@ def tile_controencodnet_pa_kernel(tc, F_, X, W1, b1, out):
 
         def round_agg(r):
             hopping = a_banks[r][:].rearrange("p t n -> p n t")
-            if r != 5:
+            if r != BLOCKS - 2:
                 nc.scalar.copy(out=a_grouped[:, r], in_=hopping)
             else:
                 nc.vector.tensor_copy(out=a_grouped[:, r], in_=hopping)
@@ -199,14 +202,15 @@ def tile_controencodnet_pa_kernel(tc, F_, X, W1, b1, out):
                 nc.scalar.activation(out=piece, in_=piece, func=TANH)
                 nc.sync.dma_start(out=out_rows[:, r, cols], in_=piece)
 
+        spread_bias()
         regroup_x(0)
+        keep_bias()
         transpose_f(0)
         quantise_x(0)
         regroup_x(1)
         quantise_f(0)
         quantise_x(1)
         transpose_f(1)
-        spread_bias()
         for r in range(2, AHEAD):
             transpose_f(r)
         for r in range(1, AHEAD):

@@ -125,6 +125,14 @@ def tile_controencodnet_pa_kernel(tc, F_, X, W1, b1, out):
                 in_=b_bank[:].rearrange("p j n -> p n j"),
             )
 
+        busy_bank = psum.tile([P, P], F32, tag="bank")
+
+        def keep_busy(count):
+            for repeat in range(count):
+                nc.tensor.matmul(
+                    out=busy_bank[:], lhsT=identity[:], rhs=identity[:], start=True, stop=True
+                )
+
         def transpose_f(r):
             words = f_in[:, r, :].bitcast(F32)
             bank = psum.tile([P, PASSES * 2, P], F32, tag="bank")
@@ -202,17 +210,21 @@ def tile_controencodnet_pa_kernel(tc, F_, X, W1, b1, out):
                 nc.scalar.activation(out=piece, in_=piece, func=TANH)
                 nc.sync.dma_start(out=out_rows[:, r, cols], in_=piece)
 
+        keep_busy(4)
         spread_bias()
         regroup_x(0)
         keep_bias()
         transpose_f(0)
+        keep_busy(3)
         quantise_x(0)
         regroup_x(1)
         quantise_f(0)
         quantise_x(1)
         transpose_f(1)
+        keep_busy(1)
         for r in range(2, AHEAD):
             transpose_f(r)
+            keep_busy(1)
         for r in range(1, AHEAD):
             quantise_f(r)
 

@@ -89,11 +89,11 @@ def tile_controencodnet_pa_kernel(tc, F_, X, W1, b1, out):
             nc.vector.quantize_mx(out=codes.bitcast(FP8X4), scales=scales, in_=grouped)
 
         def regroup_x(g):
-            grouped = x_grouped[:, g].rearrange("p (t m) j -> p t m j", t=FEAT_TILES)
-            rows = x_in[:, g].rearrange("p j (m t) -> p t m j", t=FEAT_TILES)
+            grouped = x_grouped[:, g].rearrange("p (t m) j -> p m t j", t=FEAT_TILES)
+            rows = x_in[:, g].rearrange("p j (m t) -> p m t j", t=FEAT_TILES)
             cut = P * 3 // 4
-            nc.scalar.copy(out=grouped[:, :, cut:], in_=rows[:, :, cut:])
-            nc.vector.tensor_copy(out=grouped[:, :, :cut], in_=rows[:, :, :cut])
+            nc.scalar.copy(out=grouped[:, cut:], in_=rows[:, cut:])
+            nc.vector.tensor_copy(out=grouped[:, :cut], in_=rows[:, :cut])
 
         def quantise_x(g):
             quantise(x_codes[:, g, :], x_scales[:, g, :], x_grouped[:, g].rearrange("p c t -> p (c t)"))

@@ -89,9 +89,9 @@ def tile_controencodnet_pa_kernel(tc, F_, X, W1, b1, out):
             nc.vector.quantize_mx(out=codes.bitcast(FP8X4), scales=scales, in_=grouped)
 
         def regroup_x(g):
-            grouped = x_grouped[:, g].rearrange("p (t m) j -> p m t j", t=FEAT_TILES)
-            rows = x_in[:, g].rearrange("p j (m t) -> p m t j", t=FEAT_TILES)
-            cut = P * 3 // 4
+            grouped = x_grouped[:, g].rearrange("p (t m i) j -> p m t i j", t=FEAT_TILES, i=2)
+            rows = x_in[:, g].rearrange("p j (m i t) -> p m t i j", t=FEAT_TILES, i=2)
+            cut = P * 3 // 8
             nc.scalar.copy(out=grouped[:, cut:], in_=rows[:, cut:])
             nc.vector.tensor_copy(out=grouped[:, :cut], in_=rows[:, :cut])
 
@@ -222,9 +222,10 @@ def tile_controencodnet_pa_kernel(tc, F_, X, W1, b1, out):
         quantise_x(1)
         transpose_f(1)
         keep_busy(1)
-        for r in range(2, AHEAD):
+        transpose_f(2)
+        keep_busy(1)
+        for r in range(3, AHEAD):
             transpose_f(r)
-            keep_busy(1)
         for r in range(1, AHEAD):
             quantise_f(r)
 

@@ -72,8 +72,8 @@ def tile_controencodnet_pa_kernel(tc, F_, X, W1, b1, out):
 
         load_x(0)
         load_f(0, 1)
-        load_x(1)
         load_f(1, 1)
+        load_x(1)
         load_f(2, 1)
         load_f(3, 1)
         load_f(4, 2)
@@ -215,13 +215,13 @@ def tile_controencodnet_pa_kernel(tc, F_, X, W1, b1, out):
         regroup_x(0)
         keep_bias()
         transpose_f(0)
-        keep_busy(3)
+        keep_busy(2)
         quantise_x(0)
         regroup_x(1)
         quantise_f(0)
         quantise_x(1)
         transpose_f(1)
-        keep_busy(1)
+        keep_busy(2)
         transpose_f(2)
         keep_busy(1)
         for r in range(3, AHEAD):

@@ -195,7 +195,7 @@ def tile_controencodnet_pa_kernel(tc, F_, X, W1, b1, out):
             o_banks[r] = bank
 
         def parts_of(r):
-            width = HIDDEN // 2 if r == BLOCKS - 1 else HIDDEN
+            width = HIDDEN // 2 if r >= BLOCKS - 3 else HIDDEN
             return [slice(c, c + width) for c in range(0, HIDDEN, width)]
 
         def add_bias(r):

from contextlib import ExitStack

import concourse.mybir as mybir
from concourse.masks import make_identity

F32 = mybir.dt.float32
BF16 = mybir.dt.bfloat16
U32 = mybir.dt.uint32
U8 = mybir.dt.uint8
FP8X4 = mybir.dt.float8_e4m3fn_x4
TANH = mybir.ActivationFunctionType.Tanh
ADD = mybir.AluOpType.add

P = 128
PACK = 4
K_PASS = P * PACK
NODES = 1024
FEATS = 512
HIDDEN = 512
BLOCKS = NODES // P
PASSES = NODES // K_PASS
FEAT_TILES = FEATS // P
AHEAD = 4
OUT_LAG = 3

FLOPS = 2 * NODES * NODES * FEATS + 2 * NODES * FEATS * HIDDEN


def tile_controencodnet_pa_kernel(tc, F_, X, W1, b1, out):
    nc = tc.nc
    with ExitStack() as ctx:
        keep = ctx.enter_context(tc.tile_pool(name="keep", bufs=1))
        psum = ctx.enter_context(tc.psum_pool(name="psum", bufs=8))
        ctx.enter_context(tc.manual_schedule())

        f_in = keep.tile([P, BLOCKS, NODES], BF16)
        x_in = keep.tile([P, PASSES, PACK, FEATS], BF16)
        w_in = keep.tile([P, PACK, HIDDEN], BF16)
        f_grouped = keep.tile([P, BLOCKS, PASSES * P * PACK], BF16, align_bytes=64)
        x_grouped = keep.tile([P, PASSES, FEATS, PACK], BF16, align_bytes=64)
        w_grouped = keep.tile([P, HIDDEN, PACK], BF16, align_bytes=64)
        a_grouped = keep.tile([P, BLOCKS, P, PACK], BF16, align_bytes=64)
        f_codes = keep.tile([P, BLOCKS, PASSES * P], U32, align_bytes=64)
        f_scales = keep.tile([P, BLOCKS, PASSES * P], U8, align_bytes=64)
        x_codes = keep.tile([P, PASSES, FEATS], U32, align_bytes=64)
        x_scales = keep.tile([P, PASSES, FEATS], U8, align_bytes=64)
        w_codes = keep.tile([P, HIDDEN], U32, align_bytes=64)
        w_scales = keep.tile([P, HIDDEN], U8, align_bytes=64)
        a_codes = keep.tile([P, BLOCKS, P], U32, align_bytes=64)
        a_scales = keep.tile([P, BLOCKS, P], U8, align_bytes=64)
        result = keep.tile([P, BLOCKS, HIDDEN], F32)

        identity = keep.tile([P, P], F32)
        identity_bf16 = keep.tile([P, P], BF16)
        bias_columns = keep.tile([P, PACK], BF16)
        bias_all = keep.tile([P, HIDDEN], BF16)
        warm = keep.tile([P, 1], F32)

        f_rows = F_.rearrange("(n r) k -> n r k", r=BLOCKS)
        out_rows = out.rearrange("(n r) c -> n r c", r=BLOCKS)

        nc.scalar.dma_start(out=bias_columns[:], in_=b1.rearrange("(p j) -> p j", j=PACK))

        x_rows = X.rearrange("(g p t) c -> g p t c", g=PASSES, t=PACK)

        def load_x(g):
            nc.sync.dma_start(out=x_in[:, g], in_=x_rows[g])

        def load_f(first, count):
            blocks = slice(first, first + count)
            nc.sync.dma_start(out=f_in[:, blocks, :], in_=f_rows[:, blocks, :])

        load_x(0)
        load_f(0, 1)
        load_f(1, 1)
        load_x(1)
        load_f(2, 1)
        load_f(3, 1)
        load_f(4, 2)
        nc.sync.dma_start(out=w_in[:], in_=W1.rearrange("(p t) c -> p t c", t=PACK))
        load_f(6, 2)

        nc.vector.memset(warm[:], 0.0)
        nc.scalar.activation(out=warm[:], in_=warm[:], func=TANH)
        make_identity(nc, identity[:])
        nc.vector.tensor_copy(out=identity_bf16[:], in_=identity[:])

        def quantise(codes, scales, grouped):
            nc.vector.quantize_mx(out=codes.bitcast(FP8X4), scales=scales, in_=grouped)

        def regroup_x(g):
            grouped = x_grouped[:, g].rearrange("p (t m i) j -> p m t i j", t=FEAT_TILES, i=2)
            rows = x_in[:, g].rearrange("p j (m i t) -> p m t i j", t=FEAT_TILES, i=2)
            cut = P * 3 // 8
            nc.scalar.copy(out=grouped[:, cut:], in_=rows[:, cut:])
            nc.vector.tensor_copy(out=grouped[:, :cut], in_=rows[:, :cut])

        def quantise_x(g):
            quantise(x_codes[:, g, :], x_scales[:, g, :], x_grouped[:, g].rearrange("p c t -> p (c t)"))

        def regroup_w():
            nc.vector.tensor_copy(
                out=w_grouped[:].rearrange("p (c i) t -> p c t i", i=4),
                in_=w_in[:].rearrange("p t (c i) -> p c t i", i=4),
            )

        def quantise_w():
            quantise(w_codes[:], w_scales[:], w_grouped[:].rearrange("p c t -> p (c t)"))

        b_bank = psum.tile([P, PACK, P], BF16, tag="bank")

        def spread_bias():
            for j in range(PACK):
                nc.tensor.matmul(
                    out=b_bank[:, j, :],
                    lhsT=bias_columns[:, j : j + 1].to_broadcast([P, P]),
                    rhs=identity_bf16[:],
                    start=True,
                    stop=True,
                )

        def keep_bias():
            nc.scalar.copy(
                out=bias_all[:].rearrange("p (n j) -> p n j", j=PACK),
                in_=b_bank[:].rearrange("p j n -> p n j"),
            )

        busy_bank = psum.tile([P, P], F32, tag="bank")

        def keep_busy(count):
            for repeat in range(count):
                nc.tensor.matmul(
                    out=busy_bank[:], lhsT=identity[:], rhs=identity[:], start=True, stop=True
                )

        def transpose_f(r):
            words = f_in[:, r, :].bitcast(F32)
            bank = psum.tile([P, PASSES * 2, P], F32, tag="bank")
            for g in range(PASSES):
                for u in range(2):
                    chosen = words[:, g * 2 * P + u : (g + 1) * 2 * P : 2]
                    nc.tensor.transpose(bank[:, 2 * g + u, :], chosen, identity[:])
            nc.scalar.copy(
                out=f_grouped[:, r, :].bitcast(F32).rearrange("p (g n u) -> p g n u", g=PASSES, u=2),
                in_=bank[:].rearrange("p (g u) n -> p g n u", u=2),
            )

        def quantise_f(r):
            quantise(f_codes[:, r, :], f_scales[:, r, :], f_grouped[:, r, :])

        a_banks = {}

        def aggregate(r):
            bank = psum.tile([P, FEAT_TILES, P], F32, tag="bank")
            for t in range(FEAT_TILES):
                feats = slice(t * P, (t + 1) * P)
                for g in range(PASSES):
                    nodes = slice(g * P, (g + 1) * P)
                    nc.tensor.matmul_mx(
                        out=bank[:, t, :],
                        lhsT=x_codes[:, g, feats].bitcast(FP8X4),
                        lhsT_scale=x_scales[:, g, feats],
                        rhs=f_codes[:, r, nodes].bitcast(FP8X4),
                        rhs_scale=f_scales[:, r, nodes],
                        start=(g == 0),
                        stop=(g == PASSES - 1),
                    )
            a_banks[r] = bank

        def round_agg(r):
            hopping = a_banks[r][:].rearrange("p t n -> p n t")
            if r != BLOCKS - 2:
                nc.scalar.copy(out=a_grouped[:, r], in_=hopping)
            else:
                nc.vector.tensor_copy(out=a_grouped[:, r], in_=hopping)

        def quantise_agg(r):
            quantise(
                a_codes[:, r, :], a_scales[:, r, :], a_grouped[:, r].rearrange("p n t -> p (n t)")
            )

        o_banks = {}

        def project(r):
            bank = psum.tile([P, HIDDEN], F32, tag="bank")
            nc.tensor.matmul_mx(
                out=bank[:],
                lhsT=a_codes[:, r, :].bitcast(FP8X4),
                lhsT_scale=a_scales[:, r, :],
                rhs=w_codes[:].bitcast(FP8X4),
                rhs_scale=w_scales[:],
                start=True,
                stop=True,
            )
            o_banks[r] = bank

        def parts_of(r):
            width = HIDDEN // 2 if r >= BLOCKS - 3 else HIDDEN
            return [slice(c, c + width) for c in range(0, HIDDEN, width)]

        def add_bias(r):
            for cols in parts_of(r):
                nc.vector.tensor_tensor(
                    out=result[:, r, cols], in0=o_banks[r][:, cols], in1=bias_all[:, cols], op=ADD
                )

        def finish(r):
            for cols in parts_of(r):
                piece = result[:, r, cols]
                nc.scalar.activation(out=piece, in_=piece, func=TANH)
                nc.sync.dma_start(out=out_rows[:, r, cols], in_=piece)

        keep_busy(4)
        spread_bias()
        regroup_x(0)
        keep_bias()
        transpose_f(0)
        keep_busy(2)
        quantise_x(0)
        regroup_x(1)
        quantise_f(0)
        quantise_x(1)
        transpose_f(1)
        keep_busy(2)
        transpose_f(2)
        keep_busy(1)
        for r in range(3, AHEAD):
            transpose_f(r)
        for r in range(1, AHEAD):
            quantise_f(r)

        for step in range(BLOCKS + OUT_LAG + 1):
            done = step - OUT_LAG
            if step < BLOCKS:
                aggregate(step)
                round_agg(step)
            if step in (0, 2):
                transpose_f(AHEAD + step)
                transpose_f(AHEAD + step + 1)
            if 0 <= done < BLOCKS:
                project(done)
            if step == 0:
                regroup_w()
            if 0 <= done < BLOCKS:
                add_bias(done)
            if step < BLOCKS:
                quantise_agg(step)
            if step + AHEAD < BLOCKS:
                quantise_f(step + AHEAD)
            if step == 0:
                quantise_w()
            if 0 <= done - 1 < BLOCKS:
                finish(done - 1)
